import numpy as np
import ml_dtypes


def mxq(x, axis, fmt="e4m3"):
    dtype, down = {"e4m3": (ml_dtypes.float8_e4m3fn, 7), "e5m2": (ml_dtypes.float8_e5m2, 14)}[fmt]
    v = np.moveaxis(np.asarray(x, np.float32).astype(ml_dtypes.bfloat16).astype(np.float64), axis, -1)
    blocks = v.reshape(v.shape[:-1] + (-1, 32))
    amax = np.abs(blocks).max(-1, keepdims=True)
    byte = np.maximum(np.where(amax > 0, np.frexp(amax)[1] - 1 + 127, 0) - down, 1)
    scale = np.exp2(byte - 127.0)
    codes = (blocks / scale).astype(np.float32).astype(dtype).astype(np.float64)
    return np.moveaxis((codes * scale).reshape(v.shape), -1, axis)


WIDE = False


def mx_kscale(k):
    if not WIDE:
        return np.ones(k)
    levels = np.array([10, -10, 5, -5, 0])
    a = np.random.permutation(np.resize(levels, k // 512 * 4)).reshape(k // 512, 4)
    idx = np.arange(k)
    return np.exp2(a[idx // 512, idx % 128 // 32])


BF16 = ml_dtypes.bfloat16


def bf(x):
    return np.asarray(x, np.float32).astype(BF16)


def f64(x):
    return np.asarray(x).astype(np.float64)


B, S, D, H, KVH, HD = 8, 512, 512, 4, 2, 128
E = H * HD
KV = KVH * HD
EPS = 1e-6


def layernorm(u, gamma, beta):
    mu = u.mean(-1, keepdims=True)
    var = np.square(u - mu).mean(-1, keepdims=True)
    return (u - mu) / np.sqrt(var + EPS) * gamma + beta


def apply_rope(u, cos, sin):
    half = u.shape[-1] // 2
    rotated = np.concatenate([-u[..., half:], u[..., :half]], axis=-1)
    return u * cos[None, None] + rotated * sin[None, None]


def setup_inputs():
    s = mx_kscale(D)
    return {
        "x": bf(np.random.standard_normal((B, S, D)) * s),
        "cos": bf(np.random.uniform(size=(S, HD))),
        "sin": bf(np.random.uniform(size=(S, HD))),
        "Wq": bf(np.random.standard_normal((D, E)) / np.sqrt(D) / s[:, None]),
        "Wk": bf(np.random.standard_normal((D, KV)) / np.sqrt(D) / s[:, None]),
        "Wv": bf(np.random.standard_normal((D, KV)) * 2.0 / np.sqrt(D) / s[:, None]),
        "q_gamma": bf(1.0 + 0.1 * np.random.standard_normal(HD)),
        "q_beta": bf(0.1 * np.random.standard_normal(HD)),
        "k_gamma": bf(1.0 + 0.1 * np.random.standard_normal(HD)),
        "k_beta": bf(0.1 * np.random.standard_normal(HD)),
    }


def reference(x, cos, sin, Wq, Wk, Wv, q_gamma, q_beta, k_gamma, k_beta):
    xq = mxq(f64(x), 2, "e4m3")
    q = (xq @ mxq(f64(Wq), 0, "e4m3")).reshape(B, S, H, HD).transpose(0, 2, 1, 3)
    k = (xq @ mxq(f64(Wk), 0, "e4m3")).reshape(B, S, KVH, HD).transpose(0, 2, 1, 3)
    v = (xq @ mxq(f64(Wv), 0, "e4m3")).reshape(B, S, KVH, HD).transpose(0, 2, 1, 3)
    q = layernorm(q, f64(q_gamma), f64(q_beta))
    k = layernorm(k, f64(k_gamma), f64(k_beta))
    q_rot = apply_rope(q, f64(cos), f64(sin))
    k_rot = apply_rope(k, f64(cos), f64(sin))
    return q_rot, k_rot, v

@@ -1,0 +1,285 @@
+from contextlib import ExitStack
+
+import concourse.mybir as mybir
+from concourse.masks import make_identity
+
+F32 = mybir.dt.float32
+BF16 = mybir.dt.bfloat16
+U32 = mybir.dt.uint32
+U8 = mybir.dt.uint8
+FP8X4 = mybir.dt.float8_e4m3fn_x4
+ADD = mybir.AluOpType.add
+MULT = mybir.AluOpType.mult
+ACT = mybir.ActivationFunctionType
+
+P = 128
+PACK = 4
+B, S, D = 8, 512, 512
+HD = 128
+HALF = HD // 2
+Q_HEADS, KV_HEADS = 4, 2
+NORMED = Q_HEADS + KV_HEADS
+T = S // P
+BANK = 512
+W_COLS = (Q_HEADS + 2 * KV_HEADS) * HD
+EPS = 1e-6
+
+FLOPS = 2 * B * S * D * W_COLS
+
+
+def tile_gqa_flashattn_pa_t_kernel(
+    tc, x, cos, sin, Wq, Wk, Wv, q_gamma, q_beta, k_gamma, k_beta, out_0, out_1, out_2
+):
+    nc = tc.nc
+    with ExitStack() as ctx:
+        const = ctx.enter_context(tc.tile_pool(name="const", bufs=1))
+        xprep = ctx.enter_context(tc.tile_pool(name="xprep", bufs=2))
+        stats = ctx.enter_context(tc.tile_pool(name="stats", bufs=4))
+        work = ctx.enter_context(tc.tile_pool(name="work", bufs=3))
+        outs = ctx.enter_context(tc.tile_pool(name="outs", bufs=4))
+        psum_c = ctx.enter_context(tc.psum_pool(name="psum_c", bufs=1))
+        psum_x = ctx.enter_context(tc.psum_pool(name="psum_x", bufs=2))
+        psum_u = ctx.enter_context(tc.psum_pool(name="psum_u", bufs=2))
+
+        ident = const.tile([P, P], F32)
+        make_identity(nc, ident[:])
+        ones = const.tile([P, P], BF16)
+        nc.vector.memset(ones[:], 1.0)
+        eps = const.tile([P, 1], F32)
+        nc.vector.memset(eps[:], EPS)
+        vecs = const.tile([P, 4 * HD], BF16)
+        nc.vector.memset(vecs[:], 0.0)
+
+        for n, vec in enumerate((q_gamma, k_gamma, q_beta, k_beta)):
+            nc.sync.dma_start(
+                out=vecs[0:1, n * HD : (n + 1) * HD], in_=vec.rearrange("(o j) -> o j", o=1)
+            )
+        cos_sb = const.tile([P, T, HD], BF16)
+        nc.sync.dma_start(out=cos_sb[:], in_=cos.rearrange("(p t) j -> p t j", t=T))
+        sin_sb = const.tile([P, T, HD], BF16)
+        nc.sync.dma_start(out=sin_sb[:], in_=sin.rearrange("(p t) j -> p t j", t=T))
+
+        def load_x(b):
+            x_sb = const.tile([P, T * D], BF16, name="x_sb%d" % b)
+            nc.sync.dma_start(out=x_sb[:], in_=x[b].rearrange("(p t) k -> p (t k)", t=T))
+            return x_sb
+
+        def load_w(w, name):
+            cols = w.shape[1]
+            raw = const.tile([P, PACK * cols], BF16, name=name)
+            nc.sync.dma_start(
+                out=raw[:].rearrange("p (u ec) -> p u ec", u=2),
+                in_=w.rearrange("(u p e) c -> p u (e c)", u=2, e=2),
+            )
+            return raw
+
+        x_tiles = [load_x(0)]
+        wq_raw = load_w(Wq, "wq_raw")
+        wk_raw = load_w(Wk, "wk_raw")
+        wv_raw = load_w(Wv, "wv_raw")
+        for b in range(1, B):
+            x_tiles.append(load_x(b))
+
+        def quantise_x(b):
+            x_words = x_tiles[b][:].bitcast(F32)
+            grouped = xprep.tile([P, T * P * PACK], BF16, align_bytes=64)
+            grouped_words = grouped[:].bitcast(F32)
+            for pair in range(T // 2):
+                x_t = psum_x.tile([P, BANK], F32, tag="x_t")
+                for n in range(BANK // P):
+                    nc.tensor.transpose(
+                        x_t[:, n * P : (n + 1) * P],
+                        x_words[:, pair * BANK + n * P : pair * BANK + (n + 1) * P],
+                        ident[:],
+                    )
+                nc.scalar.copy(
+                    out=grouped_words[:, pair * BANK : (pair + 1) * BANK].rearrange(
+                        "p (t r u) -> p t r u", t=2, u=2
+                    ),
+                    in_=x_t[:].rearrange("p (t u r) -> p t r u", t=2, u=2),
+                )
+            codes = xprep.tile([P, T * P], U32, align_bytes=64)
+            scales = xprep.tile([P, T * P], U8, align_bytes=64)
+            nc.vector.quantize_mx(out=codes[:].bitcast(FP8X4), scales=scales[:], in_=grouped[:])
+            return codes, scales
+
+        x_mx = quantise_x(0)
+
+        w_grouped = const.tile([P, W_COLS * PACK], BF16, align_bytes=64)
+        w_codes = const.tile([P, W_COLS], U32, align_bytes=64)
+        w_scales = const.tile([P, W_COLS], U8, align_bytes=64)
+
+        def regroup_w(copy, raw, first_col, cols):
+            copy(
+                out=w_grouped[:, first_col * PACK : (first_col + cols) * PACK].rearrange(
+                    "p (c v) -> p c v", v=PACK
+                ),
+                in_=raw[:].rearrange("p (v c) -> p c v", v=PACK),
+            )
+
+        def quantise_w(first_col, cols):
+            nc.vector.quantize_mx(
+                out=w_codes[:, first_col : first_col + cols].bitcast(FP8X4),
+                scales=w_scales[:, first_col : first_col + cols],
+                in_=w_grouped[:, first_col * PACK : (first_col + cols) * PACK],
+            )
+
+        regroup_w(nc.vector.tensor_copy, wq_raw, 0, BANK)
+        regroup_w(nc.scalar.copy, wk_raw, BANK, KV_HEADS * HD)
+        regroup_w(nc.scalar.copy, wv_raw, BANK + KV_HEADS * HD, KV_HEADS * HD)
+        quantise_w(0, BANK)
+        quantise_w(BANK, BANK)
+
+        sin_src = const.tile([P, T, HD], BF16)
+        nc.scalar.copy(out=sin_src[:, :, 0:HALF], in_=sin_sb[:, :, HALF:HD])
+        nc.scalar.mul(out=sin_src[:, :, HALF:HD], in_=sin_sb[:, :, 0:HALF], mul=-1.0)
+
+        spread = psum_x.tile([P, 4 * HD], F32, tag="x_t")
+        nc.tensor.matmul(out=spread[:], lhsT=ones[:], rhs=vecs[:], start=True, stop=True)
+
+        def scale_tables(dst, vec_pair):
+            shape = [P, T, 2, HD]
+            vec_view = vec_pair.rearrange("p (o k j) -> p o k j", o=1, k=2).to_broadcast(shape)
+            for n, table in enumerate((cos_sb, sin_src)):
+                nc.vector.tensor_tensor(
+                    out=dst[:, :, :, n, :],
+                    in0=table[:].unsqueeze(2).to_broadcast(shape),
+                    in1=vec_view,
+                    op=MULT,
+                )
+
+        def add_rotated(dst, products):
+            nc.gpsimd.tensor_tensor(
+                out=dst[:, :, 0:HALF],
+                in0=products[:, :, 0, 0:HALF],
+                in1=products[:, :, 1, HALF:HD],
+                op=ADD,
+            )
+            nc.gpsimd.tensor_tensor(
+                out=dst[:, :, HALF:HD],
+                in0=products[:, :, 0, HALF:HD],
+                in1=products[:, :, 1, 0:HALF],
+                op=ADD,
+            )
+
+        tab_ab = const.tile([P, T, 2, 2, HD], F32)
+        scale_tables(tab_ab, spread[:, 0 : 2 * HD])
+        tab_beta = const.tile([P, T, 2, 2, HD], F32)
+        scale_tables(tab_beta, spread[:, 2 * HD : 4 * HD])
+        c_sb = const.tile([P, T, 2, HD], F32)
+        add_rotated(
+            c_sb[:].rearrange("p t k j -> p (t k) j"),
+            tab_beta[:].rearrange("p t k n j -> p (t k) n j"),
+        )
+        c_ps = []
+        for pair in range(T // 2):
+            c_bank = psum_c.tile([P, 2, 2, HD], F32, name="c_bank%d" % pair)
+            nc.tensor.matmul(
+                out=c_bank[:].rearrange("p t k j -> p (t k j)"),
+                lhsT=ident[:],
+                rhs=c_sb[:, 2 * pair : 2 * pair + 2].rearrange("p t k j -> p (t k j)"),
+                start=True,
+                stop=True,
+            )
+            c_ps.append(c_bank)
+
+        def kind_of(h):
+            return 0 if h < Q_HEADS else 1
+
+        def products(b, t, x_codes, x_scales):
+            token_cols = slice(t * P, (t + 1) * P)
+            banks = []
+            for n, tag in enumerate(("u_q", "u_kv")):
+                bank = psum_u.tile([P, BANK], F32, tag=tag, name=tag)
+                nc.tensor.matmul_mx(
+                    out=bank[:],
+                    lhsT=x_codes[:, token_cols].bitcast(FP8X4),
+                    lhsT_scale=x_scales[:, token_cols],
+                    rhs=w_codes[:, n * BANK : (n + 1) * BANK].bitcast(FP8X4),
+                    rhs_scale=w_scales[:, n * BANK : (n + 1) * BANK],
+                    start=True,
+                    stop=True,
+                )
+                banks.append(bank)
+            u_kv = banks[1]
+
+            def head(h):
+                col = (h % Q_HEADS) * HD
+                return banks[kind_of(h)][:, col : col + HD]
+
+            neg_mean = stats.tile([P, NORMED], F32)
+            sum_sq = stats.tile([P, NORMED], F32)
+            unread = work.tile([P, 2 * NORMED, HD], BF16)
+            pair_ab = work.tile([P, NORMED, 2, HD], F32)
+            for heads in (range(Q_HEADS), range(Q_HEADS, NORMED)):
+                for h in heads:
+                    nc.scalar.activation(
+                        out=unread[:, h, :],
+                        in_=head(h),
+                        func=ACT.Copy,
+                        scale=-1.0 / HD,
+                        accum_out=neg_mean[:, h : h + 1],
+                    )
+                for h in heads:
+                    nc.scalar.activation(
+                        out=unread[:, NORMED + h, :],
+                        in_=head(h),
+                        func=ACT.Square,
+                        bias=neg_mean[:, h : h + 1],
+                        scale=1.0,
+                        accum_out=sum_sq[:, h : h + 1],
+                    )
+                if heads[0] == Q_HEADS:
+                    v_sb = outs.tile([P, KV_HEADS, HD], F32)
+                    nc.scalar.copy(
+                        out=v_sb[:].rearrange("p h j -> p (h j)"), in_=u_kv[:, KV_HEADS * HD : BANK]
+                    )
+                    nc.sync.dma_start(
+                        out=out_2[b].rearrange("h (p t) j -> t p h j", t=T)[t], in_=v_sb[:]
+                    )
+                for h in heads:
+                    nc.vector.scalar_tensor_tensor(
+                        out=pair_ab[:, h, :, :],
+                        in0=head(h).unsqueeze(1).to_broadcast([P, 2, HD]),
+                        scalar=neg_mean[:, h : h + 1],
+                        in1=tab_ab[:, t, kind_of(h), :, :],
+                        op0=ADD,
+                        op1=MULT,
+                    )
+            std = stats.tile([P, NORMED], F32)
+            nc.scalar.activation(
+                out=std[:], in_=sum_sq[:], func=ACT.Sqrt, bias=eps[:, 0:1], scale=1.0 / HD
+            )
+            rotated = work.tile([P, NORMED, HD], F32)
+            add_rotated(rotated, pair_ab)
+            return rotated, std
+
+        def finish(b, t, rotated, std):
+            rstd = stats.tile([P, NORMED], F32)
+            nc.vector.reciprocal(out=rstd[:], in_=std[:])
+            q_sb = outs.tile([P, Q_HEADS, HD], F32)
+            k_sb = outs.tile([P, KV_HEADS, HD], F32)
+            for h in range(NORMED):
+                dst = q_sb[:, h, :] if h < Q_HEADS else k_sb[:, h - Q_HEADS, :]
+                nc.vector.scalar_tensor_tensor(
+                    out=dst,
+                    in0=rotated[:, h, :],
+                    scalar=rstd[:, h : h + 1],
+                    in1=c_ps[t // 2][:, t % 2, kind_of(h), :],
+                    op0=MULT,
+                    op1=ADD,
+                )
+            nc.sync.dma_start(out=out_0[b].rearrange("h (p t) j -> t p h j", t=T)[t], in_=q_sb[:])
+            nc.sync.dma_start(out=out_1[b].rearrange("h (p t) j -> t p h j", t=T)[t], in_=k_sb[:])
+
+        waiting = None
+        for b in range(B):
+            x_codes, x_scales = x_mx
+            for t in range(T):
+                made = products(b, t, x_codes, x_scales)
+                if t == 0 and b + 1 < B:
+                    x_mx = quantise_x(b + 1)
+                if waiting is not None:
+                    finish(*waiting)
+                waiting = (b, t) + made
+        finish(*waiting)

@@ -7,6 +7,7 @@ F32 = mybir.dt.float32
 BF16 = mybir.dt.bfloat16
 U32 = mybir.dt.uint32
 U8 = mybir.dt.uint8
+I32 = mybir.dt.int32
 FP8X4 = mybir.dt.float8_e4m3fn_x4
 ADD = mybir.AluOpType.add
 MULT = mybir.AluOpType.mult
@@ -21,7 +22,10 @@ Q_HEADS, KV_HEADS = 4, 2
 NORMED = Q_HEADS + KV_HEADS
 T = S // P
 BANK = 512
-W_COLS = (Q_HEADS + 2 * KV_HEADS) * HD
+HEADS = Q_HEADS + 2 * KV_HEADS
+W_COLS = HEADS * HD
+FOLDS = 8
+FOLDED = HD // FOLDS
 EPS = 1e-6
 
 FLOPS = 2 * B * S * D * W_COLS
@@ -38,7 +42,8 @@ def tile_gqa_flashattn_pa_t_kernel(
         work = ctx.enter_context(tc.tile_pool(name="work", bufs=3))
         outs = ctx.enter_context(tc.tile_pool(name="outs", bufs=4))
         psum_c = ctx.enter_context(tc.psum_pool(name="psum_c", bufs=1))
-        psum_x = ctx.enter_context(tc.psum_pool(name="psum_x", bufs=2))
+        psum_x = ctx.enter_context(tc.psum_pool(name="psum_x", bufs=1))
+        psum_f = ctx.enter_context(tc.psum_pool(name="psum_f", bufs=1))
         psum_u = ctx.enter_context(tc.psum_pool(name="psum_u", bufs=2))
 
         ident = const.tile([P, P], F32)
@@ -103,11 +108,10 @@ def tile_gqa_flashattn_pa_t_kernel(
             nc.vector.quantize_mx(out=codes[:].bitcast(FP8X4), scales=scales[:], in_=grouped[:])
             return codes, scales
 
-        x_mx = quantise_x(0)
-
         w_grouped = const.tile([P, W_COLS * PACK], BF16, align_bytes=64)
         w_codes = const.tile([P, W_COLS], U32, align_bytes=64)
         w_scales = const.tile([P, W_COLS], U8, align_bytes=64)
+        nc.vector.memset(w_scales[:].bitcast(I32), 0)
 
         def regroup_w(copy, raw, first_col, cols):
             copy(
@@ -129,6 +133,45 @@ def tile_gqa_flashattn_pa_t_kernel(
         regroup_w(nc.scalar.copy, wv_raw, BANK + KV_HEADS * HD, KV_HEADS * HD)
         quantise_w(0, BANK)
         quantise_w(BANK, BANK)
+
+        fold_codes = const.tile([P, W_COLS], U32, align_bytes=64)
+        fold_scales = const.tile([P, W_COLS], U8, align_bytes=64)
+        for dst, src in ((fold_codes, w_codes), (fold_scales, w_scales)):
+            nc.vector.tensor_copy(
+                out=dst[:].bitcast(I32).rearrange("p (r h i) -> p r h i", r=FOLDS, h=HEADS),
+                in_=src[:].bitcast(I32).rearrange("p (h r i) -> p r h i", r=FOLDS, h=HEADS),
+            )
+
+        def negative_means(x_codes, x_scales):
+            folded = psum_f.tile([P, T * HEADS * FOLDED], F32)
+            for t in range(T):
+                token_cols = slice(t * P, (t + 1) * P)
+                for r in range(FOLDS):
+                    nc.tensor.matmul_mx(
+                        out=folded[:, token_cols],
+                        lhsT=x_codes[:, token_cols].bitcast(FP8X4),
+                        lhsT_scale=x_scales[:, token_cols],
+                        rhs=fold_codes[:, r * P : (r + 1) * P].bitcast(FP8X4),
+                        rhs_scale=fold_scales[:, r * P : (r + 1) * P],
+                        start=(r == 0),
+                        stop=(r == FOLDS - 1),
+                    )
+            sums = xprep.tile([P, T * HEADS], F32)
+            nc.vector.tensor_reduce(
+                out=sums[:],
+                in_=folded[:].rearrange("p (g i) -> p g i", i=FOLDED),
+                axis=mybir.AxisListType.X,
+                op=ADD,
+            )
+            neg_mean = xprep.tile([P, T * HEADS], F32)
+            nc.scalar.mul(out=neg_mean[:], in_=sums[:], mul=-1.0 / HD)
+            return neg_mean
+
+        def prepare(b):
+            x_codes, x_scales = quantise_x(b)
+            return x_codes, x_scales, negative_means(x_codes, x_scales)
+
+        following = prepare(0)
 
         sin_src = const.tile([P, T, HD], BF16)
         nc.scalar.copy(out=sin_src[:, :, 0:HALF], in_=sin_sb[:, :, HALF:HD])
@@ -186,7 +229,7 @@ def tile_gqa_flashattn_pa_t_kernel(
         def kind_of(h):
             return 0 if h < Q_HEADS else 1
 
-        def products(b, t, x_codes, x_scales):
+        def products(b, t, x_codes, x_scales, neg_means):
             token_cols = slice(t * P, (t + 1) * P)
             banks = []
             for n, tag in enumerate(("u_q", "u_kv")):
@@ -207,25 +250,19 @@ def tile_gqa_flashattn_pa_t_kernel(
                 col = (h % Q_HEADS) * HD
                 return banks[kind_of(h)][:, col : col + HD]
 
-            neg_mean = stats.tile([P, NORMED], F32)
+            def neg_mean(h):
+                return neg_means[:, t * HEADS + h : t * HEADS + h + 1]
+
             sum_sq = stats.tile([P, NORMED], F32)
-            unread = work.tile([P, 2 * NORMED, HD], BF16)
+            unread = work.tile([P, NORMED, HD], BF16)
             pair_ab = work.tile([P, NORMED, 2, HD], F32)
             for heads in (range(Q_HEADS), range(Q_HEADS, NORMED)):
                 for h in heads:
                     nc.scalar.activation(
                         out=unread[:, h, :],
                         in_=head(h),
-                        func=ACT.Copy,
-                        scale=-1.0 / HD,
-                        accum_out=neg_mean[:, h : h + 1],
-                    )
-                for h in heads:
-                    nc.scalar.activation(
-                        out=unread[:, NORMED + h, :],
-                        in_=head(h),
                         func=ACT.Square,
-                        bias=neg_mean[:, h : h + 1],
+                        bias=neg_mean(h),
                         scale=1.0,
                         accum_out=sum_sq[:, h : h + 1],
                     )
@@ -241,7 +278,7 @@ def tile_gqa_flashattn_pa_t_kernel(
                     nc.vector.scalar_tensor_tensor(
                         out=pair_ab[:, h, :, :],
                         in0=head(h).unsqueeze(1).to_broadcast([P, 2, HD]),
-                        scalar=neg_mean[:, h : h + 1],
+                        scalar=neg_mean(h),
                         in1=tab_ab[:, t, kind_of(h), :, :],
                         op0=ADD,
                         op1=MULT,
@@ -274,11 +311,11 @@ def tile_gqa_flashattn_pa_t_kernel(
 
         waiting = None
         for b in range(B):
-            x_codes, x_scales = x_mx
+            ready = following
             for t in range(T):
-                made = products(b, t, x_codes, x_scales)
+                made = products(b, t, *ready)
                 if t == 0 and b + 1 < B:
-                    x_mx = quantise_x(b + 1)
+                    following = prepare(b + 1)
                 if waiting is not None:
                     finish(*waiting)
                 waiting = (b, t) + made

@@ -7,7 +7,6 @@ F32 = mybir.dt.float32
 BF16 = mybir.dt.bfloat16
 U32 = mybir.dt.uint32
 U8 = mybir.dt.uint8
-I32 = mybir.dt.int32
 FP8X4 = mybir.dt.float8_e4m3fn_x4
 ADD = mybir.AluOpType.add
 MULT = mybir.AluOpType.mult
@@ -22,10 +21,7 @@ Q_HEADS, KV_HEADS = 4, 2
 NORMED = Q_HEADS + KV_HEADS
 T = S // P
 BANK = 512
-HEADS = Q_HEADS + 2 * KV_HEADS
-W_COLS = HEADS * HD
-FOLDS = 8
-FOLDED = HD // FOLDS
+W_COLS = (Q_HEADS + 2 * KV_HEADS) * HD
 EPS = 1e-6
 
 FLOPS = 2 * B * S * D * W_COLS
@@ -42,8 +38,7 @@ def tile_gqa_flashattn_pa_t_kernel(
         work = ctx.enter_context(tc.tile_pool(name="work", bufs=3))
         outs = ctx.enter_context(tc.tile_pool(name="outs", bufs=4))
         psum_c = ctx.enter_context(tc.psum_pool(name="psum_c", bufs=1))
-        psum_x = ctx.enter_context(tc.psum_pool(name="psum_x", bufs=1))
-        psum_f = ctx.enter_context(tc.psum_pool(name="psum_f", bufs=1))
+        psum_x = ctx.enter_context(tc.psum_pool(name="psum_x", bufs=2))
         psum_u = ctx.enter_context(tc.psum_pool(name="psum_u", bufs=2))
 
         ident = const.tile([P, P], F32)
@@ -56,13 +51,13 @@ def tile_gqa_flashattn_pa_t_kernel(
         nc.vector.memset(vecs[:], 0.0)
 
         for n, vec in enumerate((q_gamma, k_gamma, q_beta, k_beta)):
-            nc.sync.dma_start(
+            nc.scalar.dma_start(
                 out=vecs[0:1, n * HD : (n + 1) * HD], in_=vec.rearrange("(o j) -> o j", o=1)
             )
         cos_sb = const.tile([P, T, HD], BF16)
-        nc.sync.dma_start(out=cos_sb[:], in_=cos.rearrange("(p t) j -> p t j", t=T))
+        nc.scalar.dma_start(out=cos_sb[:], in_=cos.rearrange("(p t) j -> p t j", t=T))
         sin_sb = const.tile([P, T, HD], BF16)
-        nc.sync.dma_start(out=sin_sb[:], in_=sin.rearrange("(p t) j -> p t j", t=T))
+        nc.scalar.dma_start(out=sin_sb[:], in_=sin.rearrange("(p t) j -> p t j", t=T))
 
         def load_x(b):
             x_sb = const.tile([P, T * D], BF16, name="x_sb%d" % b)
@@ -89,6 +84,8 @@ def tile_gqa_flashattn_pa_t_kernel(
             x_words = x_tiles[b][:].bitcast(F32)
             grouped = xprep.tile([P, T * P * PACK], BF16, align_bytes=64)
             grouped_words = grouped[:].bitcast(F32)
+            codes = xprep.tile([P, T * P], U32, align_bytes=64)
+            scales = xprep.tile([P, T * P], U8, align_bytes=64)
             for pair in range(T // 2):
                 x_t = psum_x.tile([P, BANK], F32, tag="x_t")
                 for n in range(BANK // P):
@@ -103,15 +100,19 @@ def tile_gqa_flashattn_pa_t_kernel(
                     ),
                     in_=x_t[:].rearrange("p (t u r) -> p t r u", t=2, u=2),
                 )
-            codes = xprep.tile([P, T * P], U32, align_bytes=64)
-            scales = xprep.tile([P, T * P], U8, align_bytes=64)
-            nc.vector.quantize_mx(out=codes[:].bitcast(FP8X4), scales=scales[:], in_=grouped[:])
+                pair_cols = slice(pair * 2 * P, (pair + 1) * 2 * P)
+                nc.vector.quantize_mx(
+                    out=codes[:, pair_cols].bitcast(FP8X4),
+                    scales=scales[:, pair_cols],
+                    in_=grouped[:, pair * 2 * P * PACK : (pair + 1) * 2 * P * PACK],
+                )
             return codes, scales
+
+        x_mx = quantise_x(0)
 
         w_grouped = const.tile([P, W_COLS * PACK], BF16, align_bytes=64)
         w_codes = const.tile([P, W_COLS], U32, align_bytes=64)
         w_scales = const.tile([P, W_COLS], U8, align_bytes=64)
-        nc.vector.memset(w_scales[:].bitcast(I32), 0)
 
         def regroup_w(copy, raw, first_col, cols):
             copy(
@@ -133,45 +134,6 @@ def tile_gqa_flashattn_pa_t_kernel(
         regroup_w(nc.scalar.copy, wv_raw, BANK + KV_HEADS * HD, KV_HEADS * HD)
         quantise_w(0, BANK)
         quantise_w(BANK, BANK)
-
-        fold_codes = const.tile([P, W_COLS], U32, align_bytes=64)
-        fold_scales = const.tile([P, W_COLS], U8, align_bytes=64)
-        for dst, src in ((fold_codes, w_codes), (fold_scales, w_scales)):
-            nc.vector.tensor_copy(
-                out=dst[:].bitcast(I32).rearrange("p (r h i) -> p r h i", r=FOLDS, h=HEADS),
-                in_=src[:].bitcast(I32).rearrange("p (h r i) -> p r h i", r=FOLDS, h=HEADS),
-            )
-
-        def negative_means(x_codes, x_scales):
-            folded = psum_f.tile([P, T * HEADS * FOLDED], F32)
-            for t in range(T):
-                token_cols = slice(t * P, (t + 1) * P)
-                for r in range(FOLDS):
-                    nc.tensor.matmul_mx(
-                        out=folded[:, token_cols],
-                        lhsT=x_codes[:, token_cols].bitcast(FP8X4),
-                        lhsT_scale=x_scales[:, token_cols],
-                        rhs=fold_codes[:, r * P : (r + 1) * P].bitcast(FP8X4),
-                        rhs_scale=fold_scales[:, r * P : (r + 1) * P],
-                        start=(r == 0),
-                        stop=(r == FOLDS - 1),
-                    )
-            sums = xprep.tile([P, T * HEADS], F32)
-            nc.vector.tensor_reduce(
-                out=sums[:],
-                in_=folded[:].rearrange("p (g i) -> p g i", i=FOLDED),
-                axis=mybir.AxisListType.X,
-                op=ADD,
-            )
-            neg_mean = xprep.tile([P, T * HEADS], F32)
-            nc.scalar.mul(out=neg_mean[:], in_=sums[:], mul=-1.0 / HD)
-            return neg_mean
-
-        def prepare(b):
-            x_codes, x_scales = quantise_x(b)
-            return x_codes, x_scales, negative_means(x_codes, x_scales)
-
-        following = prepare(0)
 
         sin_src = const.tile([P, T, HD], BF16)
         nc.scalar.copy(out=sin_src[:, :, 0:HALF], in_=sin_sb[:, :, HALF:HD])
@@ -229,7 +191,7 @@ def tile_gqa_flashattn_pa_t_kernel(
         def kind_of(h):
             return 0 if h < Q_HEADS else 1
 
-        def products(b, t, x_codes, x_scales, neg_means):
+        def products(b, t, x_codes, x_scales):
             token_cols = slice(t * P, (t + 1) * P)
             banks = []
             for n, tag in enumerate(("u_q", "u_kv")):
@@ -250,19 +212,25 @@ def tile_gqa_flashattn_pa_t_kernel(
                 col = (h % Q_HEADS) * HD
                 return banks[kind_of(h)][:, col : col + HD]
 
-            def neg_mean(h):
-                return neg_means[:, t * HEADS + h : t * HEADS + h + 1]
-
+            neg_mean = stats.tile([P, NORMED], F32)
             sum_sq = stats.tile([P, NORMED], F32)
-            unread = work.tile([P, NORMED, HD], BF16)
+            unread = work.tile([P, 2 * NORMED, HD], BF16)
             pair_ab = work.tile([P, NORMED, 2, HD], F32)
             for heads in (range(Q_HEADS), range(Q_HEADS, NORMED)):
                 for h in heads:
                     nc.scalar.activation(
                         out=unread[:, h, :],
                         in_=head(h),
+                        func=ACT.Copy,
+                        scale=-1.0 / HD,
+                        accum_out=neg_mean[:, h : h + 1],
+                    )
+                for h in heads:
+                    nc.scalar.activation(
+                        out=unread[:, NORMED + h, :],
+                        in_=head(h),
                         func=ACT.Square,
-                        bias=neg_mean(h),
+                        bias=neg_mean[:, h : h + 1],
                         scale=1.0,
                         accum_out=sum_sq[:, h : h + 1],
                     )
@@ -278,22 +246,24 @@ def tile_gqa_flashattn_pa_t_kernel(
                     nc.vector.scalar_tensor_tensor(
                         out=pair_ab[:, h, :, :],
                         in0=head(h).unsqueeze(1).to_broadcast([P, 2, HD]),
-                        scalar=neg_mean(h),
+                        scalar=neg_mean[:, h : h + 1],
                         in1=tab_ab[:, t, kind_of(h), :, :],
                         op0=ADD,
                         op1=MULT,
                     )
-            std = stats.tile([P, NORMED], F32)
+            rstd = stats.tile([P, NORMED], F32)
             nc.scalar.activation(
-                out=std[:], in_=sum_sq[:], func=ACT.Sqrt, bias=eps[:, 0:1], scale=1.0 / HD
+                out=rstd[:],
+                in_=sum_sq[:],
+                func=ACT.Abs_reciprocal_sqrt,
+                bias=eps[:, 0:1],
+                scale=1.0 / HD,
             )
             rotated = work.tile([P, NORMED, HD], F32)
             add_rotated(rotated, pair_ab)
-            return rotated, std
+            return rotated, rstd
 
-        def finish(b, t, rotated, std):
-            rstd = stats.tile([P, NORMED], F32)
-            nc.vector.reciprocal(out=rstd[:], in_=std[:])
+        def finish(b, t, rotated, rstd):
             q_sb = outs.tile([P, Q_HEADS, HD], F32)
             k_sb = outs.tile([P, KV_HEADS, HD], F32)
             for h in range(NORMED):
@@ -311,11 +281,11 @@ def tile_gqa_flashattn_pa_t_kernel(
 
         waiting = None
         for b in range(B):
-            ready = following
+            x_codes, x_scales = x_mx
             for t in range(T):
-                made = products(b, t, *ready)
+                made = products(b, t, x_codes, x_scales)
                 if t == 0 and b + 1 < B:
-                    following = prepare(b + 1)
+                    x_mx = quantise_x(b + 1)
                 if waiting is not None:
                     finish(*waiting)
                 waiting = (b, t) + made

from contextlib import ExitStack

import concourse.mybir as mybir
from concourse.masks import make_identity

F32 = mybir.dt.float32
BF16 = mybir.dt.bfloat16
U32 = mybir.dt.uint32
U8 = mybir.dt.uint8
FP8X4 = mybir.dt.float8_e4m3fn_x4
ADD = mybir.AluOpType.add
MULT = mybir.AluOpType.mult
ACT = mybir.ActivationFunctionType

P = 128
PACK = 4
B, S, D = 8, 512, 512
HD = 128
HALF = HD // 2
Q_HEADS, KV_HEADS = 4, 2
NORMED = Q_HEADS + KV_HEADS
T = S // P
BANK = 512
W_COLS = (Q_HEADS + 2 * KV_HEADS) * HD
EPS = 1e-6

FLOPS = 2 * B * S * D * W_COLS


def tile_gqa_flashattn_pa_t_kernel(
    tc, x, cos, sin, Wq, Wk, Wv, q_gamma, q_beta, k_gamma, k_beta, out_0, out_1, out_2
):
    nc = tc.nc
    with ExitStack() as ctx:
        const = ctx.enter_context(tc.tile_pool(name="const", bufs=1))
        xprep = ctx.enter_context(tc.tile_pool(name="xprep", bufs=2))
        stats = ctx.enter_context(tc.tile_pool(name="stats", bufs=4))
        work = ctx.enter_context(tc.tile_pool(name="work", bufs=3))
        outs = ctx.enter_context(tc.tile_pool(name="outs", bufs=4))
        psum_c = ctx.enter_context(tc.psum_pool(name="psum_c", bufs=1))
        psum_x = ctx.enter_context(tc.psum_pool(name="psum_x", bufs=2))
        psum_u = ctx.enter_context(tc.psum_pool(name="psum_u", bufs=2))

        ident = const.tile([P, P], F32)
        make_identity(nc, ident[:])
        ones = const.tile([P, P], BF16)
        nc.vector.memset(ones[:], 1.0)
        eps = const.tile([P, 1], F32)
        nc.vector.memset(eps[:], EPS)
        vecs = const.tile([P, 4 * HD], BF16)
        nc.vector.memset(vecs[:], 0.0)

        for n, vec in enumerate((q_gamma, k_gamma, q_beta, k_beta)):
            nc.scalar.dma_start(
                out=vecs[0:1, n * HD : (n + 1) * HD], in_=vec.rearrange("(o j) -> o j", o=1)
            )
        cos_sb = const.tile([P, T, HD], BF16)
        nc.scalar.dma_start(out=cos_sb[:], in_=cos.rearrange("(p t) j -> p t j", t=T))
        sin_sb = const.tile([P, T, HD], BF16)
        nc.scalar.dma_start(out=sin_sb[:], in_=sin.rearrange("(p t) j -> p t j", t=T))

        def load_x(b):
            x_sb = const.tile([P, T * D], BF16, name="x_sb%d" % b)
            nc.sync.dma_start(out=x_sb[:], in_=x[b].rearrange("(p t) k -> p (t k)", t=T))
            return x_sb

        def load_w(w, name):
            cols = w.shape[1]
            raw = const.tile([P, PACK * cols], BF16, name=name)
            nc.sync.dma_start(
                out=raw[:].rearrange("p (u ec) -> p u ec", u=2),
                in_=w.rearrange("(u p e) c -> p u (e c)", u=2, e=2),
            )
            return raw

        x_tiles = [load_x(0)]
        wq_raw = load_w(Wq, "wq_raw")
        wk_raw = load_w(Wk, "wk_raw")
        wv_raw = load_w(Wv, "wv_raw")
        for b in range(1, B):
            x_tiles.append(load_x(b))

        def quantise_x(b):
            x_words = x_tiles[b][:].bitcast(F32)
            grouped = xprep.tile([P, T * P * PACK], BF16, align_bytes=64)
            grouped_words = grouped[:].bitcast(F32)
            codes = xprep.tile([P, T * P], U32, align_bytes=64)
            scales = xprep.tile([P, T * P], U8, align_bytes=64)
            for pair in range(T // 2):
                x_t = psum_x.tile([P, BANK], F32, tag="x_t")
                for n in range(BANK // P):
                    nc.tensor.transpose(
                        x_t[:, n * P : (n + 1) * P],
                        x_words[:, pair * BANK + n * P : pair * BANK + (n + 1) * P],
                        ident[:],
                    )
                nc.scalar.copy(
                    out=grouped_words[:, pair * BANK : (pair + 1) * BANK].rearrange(
                        "p (t r u) -> p t r u", t=2, u=2
                    ),
                    in_=x_t[:].rearrange("p (t u r) -> p t r u", t=2, u=2),
                )
                pair_cols = slice(pair * 2 * P, (pair + 1) * 2 * P)
                nc.vector.quantize_mx(
                    out=codes[:, pair_cols].bitcast(FP8X4),
                    scales=scales[:, pair_cols],
                    in_=grouped[:, pair * 2 * P * PACK : (pair + 1) * 2 * P * PACK],
                )
            return codes, scales

        x_mx = quantise_x(0)

        w_grouped = const.tile([P, W_COLS * PACK], BF16, align_bytes=64)
        w_codes = const.tile([P, W_COLS], U32, align_bytes=64)
        w_scales = const.tile([P, W_COLS], U8, align_bytes=64)

        def regroup_w(copy, raw, first_col, cols):
            copy(
                out=w_grouped[:, first_col * PACK : (first_col + cols) * PACK].rearrange(
                    "p (c v) -> p c v", v=PACK
                ),
                in_=raw[:].rearrange("p (v c) -> p c v", v=PACK),
            )

        def quantise_w(first_col, cols):
            nc.vector.quantize_mx(
                out=w_codes[:, first_col : first_col + cols].bitcast(FP8X4),
                scales=w_scales[:, first_col : first_col + cols],
                in_=w_grouped[:, first_col * PACK : (first_col + cols) * PACK],
            )

        regroup_w(nc.vector.tensor_copy, wq_raw, 0, BANK)
        regroup_w(nc.scalar.copy, wk_raw, BANK, KV_HEADS * HD)
        regroup_w(nc.scalar.copy, wv_raw, BANK + KV_HEADS * HD, KV_HEADS * HD)
        quantise_w(0, BANK)
        quantise_w(BANK, BANK)

        sin_src = const.tile([P, T, HD], BF16)
        nc.scalar.copy(out=sin_src[:, :, 0:HALF], in_=sin_sb[:, :, HALF:HD])
        nc.scalar.mul(out=sin_src[:, :, HALF:HD], in_=sin_sb[:, :, 0:HALF], mul=-1.0)

        spread = psum_x.tile([P, 4 * HD], F32, tag="x_t")
        nc.tensor.matmul(out=spread[:], lhsT=ones[:], rhs=vecs[:], start=True, stop=True)

        def scale_tables(dst, vec_pair):
            shape = [P, T, 2, HD]
            vec_view = vec_pair.rearrange("p (o k j) -> p o k j", o=1, k=2).to_broadcast(shape)
            for n, table in enumerate((cos_sb, sin_src)):
                nc.vector.tensor_tensor(
                    out=dst[:, :, :, n, :],
                    in0=table[:].unsqueeze(2).to_broadcast(shape),
                    in1=vec_view,
                    op=MULT,
                )

        def add_rotated(dst, products):
            nc.gpsimd.tensor_tensor(
                out=dst[:, :, 0:HALF],
                in0=products[:, :, 0, 0:HALF],
                in1=products[:, :, 1, HALF:HD],
                op=ADD,
            )
            nc.gpsimd.tensor_tensor(
                out=dst[:, :, HALF:HD],
                in0=products[:, :, 0, HALF:HD],
                in1=products[:, :, 1, 0:HALF],
                op=ADD,
            )

        tab_ab = const.tile([P, T, 2, 2, HD], F32)
        scale_tables(tab_ab, spread[:, 0 : 2 * HD])
        tab_beta = const.tile([P, T, 2, 2, HD], F32)
        scale_tables(tab_beta, spread[:, 2 * HD : 4 * HD])
        c_sb = const.tile([P, T, 2, HD], F32)
        add_rotated(
            c_sb[:].rearrange("p t k j -> p (t k) j"),
            tab_beta[:].rearrange("p t k n j -> p (t k) n j"),
        )
        c_ps = []
        for pair in range(T // 2):
            c_bank = psum_c.tile([P, 2, 2, HD], F32, name="c_bank%d" % pair)
            nc.tensor.matmul(
                out=c_bank[:].rearrange("p t k j -> p (t k j)"),
                lhsT=ident[:],
                rhs=c_sb[:, 2 * pair : 2 * pair + 2].rearrange("p t k j -> p (t k j)"),
                start=True,
                stop=True,
            )
            c_ps.append(c_bank)

        def kind_of(h):
            return 0 if h < Q_HEADS else 1

        def products(b, t, x_codes, x_scales):
            token_cols = slice(t * P, (t + 1) * P)
            banks = []
            for n, tag in enumerate(("u_q", "u_kv")):
                bank = psum_u.tile([P, BANK], F32, tag=tag, name=tag)
                nc.tensor.matmul_mx(
                    out=bank[:],
                    lhsT=x_codes[:, token_cols].bitcast(FP8X4),
                    lhsT_scale=x_scales[:, token_cols],
                    rhs=w_codes[:, n * BANK : (n + 1) * BANK].bitcast(FP8X4),
                    rhs_scale=w_scales[:, n * BANK : (n + 1) * BANK],
                    start=True,
                    stop=True,
                )
                banks.append(bank)
            u_kv = banks[1]

            def head(h):
                col = (h % Q_HEADS) * HD
                return banks[kind_of(h)][:, col : col + HD]

            neg_mean = stats.tile([P, NORMED], F32)
            sum_sq = stats.tile([P, NORMED], F32)
            unread = work.tile([P, 2 * NORMED, HD], BF16)
            pair_ab = work.tile([P, NORMED, 2, HD], F32)
            for heads in (range(Q_HEADS), range(Q_HEADS, NORMED)):
                for h in heads:
                    nc.scalar.activation(
                        out=unread[:, h, :],
                        in_=head(h),
                        func=ACT.Copy,
                        scale=-1.0 / HD,
                        accum_out=neg_mean[:, h : h + 1],
                    )
                for h in heads:
                    nc.scalar.activation(
                        out=unread[:, NORMED + h, :],
                        in_=head(h),
                        func=ACT.Square,
                        bias=neg_mean[:, h : h + 1],
                        scale=1.0,
                        accum_out=sum_sq[:, h : h + 1],
                    )
                if heads[0] == Q_HEADS:
                    v_sb = outs.tile([P, KV_HEADS, HD], F32)
                    nc.scalar.copy(
                        out=v_sb[:].rearrange("p h j -> p (h j)"), in_=u_kv[:, KV_HEADS * HD : BANK]
                    )
                    nc.sync.dma_start(
                        out=out_2[b].rearrange("h (p t) j -> t p h j", t=T)[t], in_=v_sb[:]
                    )
                for h in heads:
                    nc.vector.scalar_tensor_tensor(
                        out=pair_ab[:, h, :, :],
                        in0=head(h).unsqueeze(1).to_broadcast([P, 2, HD]),
                        scalar=neg_mean[:, h : h + 1],
                        in1=tab_ab[:, t, kind_of(h), :, :],
                        op0=ADD,
                        op1=MULT,
                    )
            rstd = stats.tile([P, NORMED], F32)
            nc.scalar.activation(
                out=rstd[:],
                in_=sum_sq[:],
                func=ACT.Abs_reciprocal_sqrt,
                bias=eps[:, 0:1],
                scale=1.0 / HD,
            )
            rotated = work.tile([P, NORMED, HD], F32)
            add_rotated(rotated, pair_ab)
            return rotated, rstd

        def finish(b, t, rotated, rstd):
            q_sb = outs.tile([P, Q_HEADS, HD], F32)
            k_sb = outs.tile([P, KV_HEADS, HD], F32)
            for h in range(NORMED):
                dst = q_sb[:, h, :] if h < Q_HEADS else k_sb[:, h - Q_HEADS, :]
                nc.vector.scalar_tensor_tensor(
                    out=dst,
                    in0=rotated[:, h, :],
                    scalar=rstd[:, h : h + 1],
                    in1=c_ps[t // 2][:, t % 2, kind_of(h), :],
                    op0=MULT,
                    op1=ADD,
                )
            nc.sync.dma_start(out=out_0[b].rearrange("h (p t) j -> t p h j", t=T)[t], in_=q_sb[:])
            nc.sync.dma_start(out=out_1[b].rearrange("h (p t) j -> t p h j", t=T)[t], in_=k_sb[:])

        waiting = None
        for b in range(B):
            x_codes, x_scales = x_mx
            for t in range(T):
                made = products(b, t, x_codes, x_scales)
                if t == 0 and b + 1 < B:
                    x_mx = quantise_x(b + 1)
                if waiting is not None:
                    finish(*waiting)
                waiting = (b, t) + made
        finish(*waiting)
